import numpy as np
import ml_dtypes


def mxq(x, axis, fmt="e4m3"):
    dtype, down = {"e4m3": (ml_dtypes.float8_e4m3fn, 7), "e5m2": (ml_dtypes.float8_e5m2, 14)}[fmt]
    v = np.moveaxis(np.asarray(x, np.float32).astype(ml_dtypes.bfloat16).astype(np.float64), axis, -1)
    blocks = v.reshape(v.shape[:-1] + (-1, 32))
    amax = np.abs(blocks).max(-1, keepdims=True)
    byte = np.maximum(np.where(amax > 0, np.frexp(amax)[1] - 1 + 127, 0) - down, 1)
    scale = np.exp2(byte - 127.0)
    codes = (blocks / scale).astype(np.float32).astype(dtype).astype(np.float64)
    return np.moveaxis((codes * scale).reshape(v.shape), -1, axis)


WIDE = False


def mx_kscale(k):
    if not WIDE:
        return np.ones(k)
    levels = np.array([10, -10, 5, -5, 0])
    a = np.random.permutation(np.resize(levels, k // 512 * 4)).reshape(k // 512, 4)
    idx = np.arange(k)
    return np.exp2(a[idx // 512, idx % 128 // 32])


BF16 = ml_dtypes.bfloat16


def bf(x):
    return np.asarray(x, np.float32).astype(BF16)


def f64(x):
    return np.asarray(x).astype(np.float64)


E2M1 = np.array([0.0, 0.5, 1.0, 1.5, 2.0, 3.0, 4.0, 6.0, -0.0, -0.5, -1.0, -1.5, -2.0, -3.0, -4.0, -6.0])


def pack_weight(w, fmt):
    k, n = w.shape
    w = f64(bf(w)).reshape(k // 32, 32, n)
    amax = np.abs(w).max(1)
    if fmt == "e4m3":
        byte = np.frexp(amax)[1] - 1 + 127 - 7
    else:
        mant, ex = np.frexp(amax / 6.0)
        byte = np.where(mant > 0.5, ex, ex - 1) + 127
    byte = np.clip(np.where(amax > 0, byte, 1), 1, 254)
    scaled = (w * np.exp2(127.0 - byte)[:, None, :]).reshape(k, n).astype(np.float32)
    by_word = np.ascontiguousarray(scaled.reshape(k // 512, 128, 4, n).transpose(0, 1, 3, 2))
    if fmt == "e4m3":
        words = by_word.astype(ml_dtypes.float8_e4m3fn).view(np.uint8)
    else:
        c = by_word.astype(ml_dtypes.float4_e2m1fn).view(np.uint8) & 0xF
        words = c[..., 0::2] | (c[..., 1::2] << 4)
    return np.ascontiguousarray(words), np.ascontiguousarray(byte.astype(np.uint8).reshape(k // 512, 16, n))


def unpack_weight(words, scales, fmt):
    g, p, n, _ = words.shape
    if fmt == "e4m3":
        vals = np.ascontiguousarray(words).view(ml_dtypes.float8_e4m3fn).astype(np.float64)
    else:
        nib = np.empty((g, p, n, 4), np.uint8)
        nib[..., 0::2] = words & 0xF
        nib[..., 1::2] = words >> 4
        vals = E2M1[nib]
    vals = vals * np.repeat(np.exp2(scales.astype(np.float64) - 127.0), 8, axis=1)[..., None]
    return vals.transpose(0, 1, 3, 2).reshape(g * 512, n)


B, I, H = 128, 4096, 1024
FMT = "e4m3"


def sigmoid(v):
    return 1.0 / (1.0 + np.exp(-v))


def setup_inputs():
    s = mx_kscale(I)
    x = bf(np.random.standard_normal((B, I)) * s)
    h_prev = bf(np.random.standard_normal((B, H)))
    c_prev = bf(np.random.standard_normal((B, H)))
    w_ih = np.random.standard_normal((4 * H, I)) * 1.0 / np.sqrt(I) / s[None, :]
    w_ih_words, w_ih_scales = pack_weight(np.ascontiguousarray(w_ih.T), FMT)
    w_hh = bf(np.random.standard_normal((4 * H, H)) * 1.0 / np.sqrt(H))
    bias_ih = bf(np.random.standard_normal(4 * H) * 0.5)
    bias_hh = bf(np.random.standard_normal(4 * H) * 0.5)
    return {"x": x,
            "h_prev": h_prev,
            "c_prev": c_prev,
            "w_ih_words": w_ih_words,
            "w_ih_scales": w_ih_scales,
            "w_hh": w_hh,
            "bias_ih": bias_ih,
            "bias_hh": bias_hh}


def reference(x, h_prev, c_prev, w_ih_words, w_ih_scales, w_hh, bias_ih, bias_hh):
    gates = (mxq(f64(x), 1, "e4m3") @ unpack_weight(w_ih_words, w_ih_scales, FMT)) + f64(bias_ih) + f64(h_prev) @ f64(w_hh).T + f64(bias_hh)
    i_g, f_g, g_g, o_g = np.split(gates, 4, axis=1)
    i_g = sigmoid(i_g)
    f_g = sigmoid(f_g)
    g_g = np.tanh(g_g)
    o_g = sigmoid(o_g)
    c_new = f_g * f64(c_prev) + i_g * g_g
    h_new = o_g * np.tanh(c_new)
    return (h_new, c_new)

@@ -1,0 +1,282 @@
+from contextlib import ExitStack
+
+import concourse.mybir as mybir
+from concourse.masks import make_identity
+
+F32 = mybir.dt.float32
+BF16 = mybir.dt.bfloat16
+I32 = mybir.dt.int32
+U32 = mybir.dt.uint32
+U8 = mybir.dt.uint8
+FP8X4 = mybir.dt.float8_e4m3fn_x4
+ACT = mybir.ActivationFunctionType
+ALU = mybir.AluOpType
+
+P = 128
+BATCH = 128
+IN = 4096
+HID = 1024
+GATES = 4
+PASSES = IN // 512
+BANK = 512
+FLOPS = 2 * BATCH * (IN + HID) * GATES * HID
+
+MANUAL = True
+
+
+def tile_int8lstmcell_w_kernel(
+    tc, x, h_prev, c_prev, w_ih_words, w_ih_scales, w_hh, bias_ih, bias_hh, out_0, out_1
+):
+    nc = tc.nc
+    with ExitStack() as stack:
+        if MANUAL:
+            stack.enter_context(tc.manual_schedule())
+        keep = stack.enter_context(tc.tile_pool(name="keep", bufs=1))
+        big = stack.enter_context(tc.tile_pool(name="big", bufs=8))
+        turned = stack.enter_context(tc.tile_pool(name="turned", bufs=5))
+        work = stack.enter_context(tc.tile_pool(name="work", bufs=3))
+        psum = stack.enter_context(tc.psum_pool(name="psum", bufs=4))
+
+        planes = keep.tile([P, 2, IN], U8, name="planes", align_bytes=64)
+        nc.vector.memset(planes[:].rearrange("p t n -> p (t n)").bitcast(I32), 0)
+        bias_rows = keep.tile([P, BANK], BF16, name="bias_rows")
+        nc.vector.memset(bias_rows[:], 0.0)
+        ident = keep.tile([P, P], F32, name="ident")
+        make_identity(nc, ident[:])
+        pick = keep.tile([P, 8], BF16, name="pick")
+        nc.vector.tensor_tensor(out=pick[:], in0=ident[:, 0:8], in1=ident[:, 8:16], op=ALU.add)
+
+        h_sb = keep.tile([P, HID], BF16, name="h_sb")
+        nc.sync.dma_start(out=h_sb[:], in_=h_prev)
+        x_sb = big.tile([P, IN], BF16, name="x_sb", tag="big", align_bytes=64)
+        nc.sync.dma_start(out=x_sb[:], in_=x)
+        nc.sync.dma_start(out=bias_rows[0:8, :], in_=bias_ih.rearrange("(j n) -> j n", j=8))
+        nc.sync.dma_start(out=bias_rows[8:16, :], in_=bias_hh.rearrange("(j n) -> j n", j=8))
+        scale_words = w_ih_scales.bitcast(I32)
+        for t in range(2):
+            for q in range(4):
+                nc.sync.dma_start(
+                    out=planes[32 * q : 32 * q + 16, t, :].bitcast(I32),
+                    in_=scale_words[4 * t : 4 * t + 4, 4 * q : 4 * q + 4, :],
+                )
+        w_words = []
+        for gate in range(GATES):
+            w_nat = big.tile([P, 8 * HID], BF16, name="w_nat", tag="big", align_bytes=64)
+            nc.sync.dma_start(
+                out=w_nat[:],
+                in_=w_hh[gate * HID : (gate + 1) * HID, :].rearrange("(p a) k -> p (a k)", a=8),
+            )
+            w_words.append(w_nat[:].bitcast(F32))
+        c_sb = keep.tile([P, HID], BF16, name="c_sb")
+        nc.sync.dma_start(out=c_sb[:], in_=c_prev)
+
+        ww = w_ih_words.rearrange("g p n t -> g p (n t)").bitcast(I32)
+
+        def load_w(dst, first_local, first_pass, n_pass, col, n_col):
+            nc.sync.dma_start(
+                out=dst[:, first_local : first_local + n_pass, :].bitcast(I32),
+                in_=ww[first_pass : first_pass + n_pass, :, col : col + n_col].rearrange("g p n -> p g n"),
+            )
+
+        w_if = []
+
+        def load_if(j):
+            dst = big.tile([P, 2, 2 * HID], U32, name="w_if", tag="big", align_bytes=64)
+            load_w(dst, 0, 2 * j, 1, 0, 2 * HID)
+            load_w(dst, 1, 2 * j + 1, 1, 0, 2 * HID)
+            w_if.append(dst)
+
+        w_go = {}
+
+        def load_gate(gate, j, cuts):
+            dst = big.tile([P, 4, HID], U32, name="w_go", tag="big", align_bytes=64)
+            first = 0
+            for n_pass in cuts:
+                load_w(dst, first, 4 * j + first, n_pass, gate * HID, HID)
+                first += n_pass
+            w_go[(gate, j)] = dst
+
+        for j in range(3):
+            load_if(j)
+
+        h_words = h_sb[:].bitcast(F32)
+        h_bank = psum.tile([P, 4, P], F32, name="h_bank", tag="tp")
+        for u in range(4):
+            nc.tensor.transpose(out=h_bank[:, u, :], in_=h_words[:, P * u : P * (u + 1)], identity=ident[:])
+        h_t = keep.tile([P, 4, 2, P], BF16, name="h_t")
+        nc.vector.tensor_copy(
+            out=h_t[:],
+            in_=h_bank[:].rearrange("q u b -> q (u b)").bitcast(BF16).rearrange("q (u b e) -> q u e b", u=4, e=2),
+        )
+
+        x_words = x_sb[:].bitcast(F32)
+        x_codes = keep.tile([P, PASSES * P], U32, name="x_codes", align_bytes=64)
+        x_scales = keep.tile([P, PASSES * P], U8, name="x_scales", align_bytes=64)
+        grouped = []
+        for half in range(2):
+            grp = turned.tile([P, 4, P, 2], F32, name="grp", tag="turned", align_bytes=64)
+            for pair in range(2):
+                x_bank = psum.tile([P, 2, 2, P], F32, name="x_bank", tag="tp")
+                for gl in range(2):
+                    g = 4 * half + 2 * pair + gl
+                    for u in range(2):
+                        nc.tensor.transpose(
+                            out=x_bank[:, gl, u, :],
+                            in_=x_words[:, 256 * g + u : 256 * (g + 1) : 2],
+                            identity=ident[:],
+                        )
+                copy = nc.vector.tensor_copy if pair == 0 else nc.scalar.copy
+                copy(out=grp[:, 2 * pair : 2 * pair + 2, :, :], in_=x_bank[:].rearrange("p g u b -> p g b u"))
+            grouped.append(grp)
+        for half in range(2):
+            nc.vector.quantize_mx(
+                out=x_codes[:, 512 * half : 512 * (half + 1)].bitcast(FP8X4),
+                scales=x_scales[:, 512 * half : 512 * (half + 1)],
+                in_=grouped[half][:].rearrange("p g b u -> p (g b u)").bitcast(BF16),
+            )
+        load_if(3)
+
+        hh_sb = keep.tile([P, GATES * HID], F32, name="hh_sb")
+        w_t = {}
+        hh = {}
+
+        def transpose_steps(unit):
+            gate, u = divmod(unit, 4)
+            copy = nc.vector.tensor_copy if unit % 2 == 0 else nc.scalar.copy
+            state = {}
+
+            def step(half, a):
+                def run():
+                    if half == 0 and a == 0:
+                        w_t[unit] = turned.tile([P, P, 8], F32, name="w_t", tag="turned", align_bytes=64)
+                    if a == 0:
+                        state["bank"] = psum.tile([P, 4, P], F32, name="w_bank", tag="tp")
+                    first = (4 * half + a) * (HID // 2) + P * u
+                    nc.tensor.transpose(
+                        out=state["bank"][:, a, :], in_=w_words[gate][:, first : first + P], identity=ident[:]
+                    )
+                    if a == 3:
+                        copy(
+                            out=w_t[unit][:, :, 4 * half : 4 * half + 4],
+                            in_=state["bank"][:].rearrange("q a p -> q p a"),
+                        )
+
+                return run
+
+            return [step(half, a) for half in range(2) for a in range(4)]
+
+        def matmul_steps(unit):
+            gate, u = divmod(unit, 4)
+
+            def step(e, nb):
+                def run():
+                    pairs = w_t[unit][:].rearrange("q p a -> q (p a)").bitcast(BF16)
+                    nc.tensor.matmul(
+                        out=hh[(gate, nb)][:],
+                        lhsT=h_t[:, u, e, :],
+                        rhs=pairs.rearrange("q (n e) -> q n e", e=2)[:, nb * BANK : (nb + 1) * BANK, e],
+                        start=False,
+                        stop=(u == 3 and e == 1),
+                    )
+
+                return run
+
+            return [step(e, nb) for e in range(2) for nb in range(2)]
+
+        for unit in range(2):
+            for run in transpose_steps(unit):
+                run()
+        for unit in range(4 * GATES):
+            gate, u = divmod(unit, 4)
+            if u == 0:
+                for nb in range(2):
+                    hh[(gate, nb)] = psum.tile([P, BANK], F32, name="hh", tag="acc")
+                    j = 2 * gate + nb
+                    nc.tensor.matmul(
+                        out=hh[(gate, nb)][:],
+                        lhsT=pick[:, j : j + 1].to_broadcast([P, P]),
+                        rhs=bias_rows[:],
+                        start=True,
+                        stop=False,
+                    )
+            ahead = transpose_steps(unit + 2) if unit + 2 < 4 * GATES else []
+            for i, run in enumerate(matmul_steps(unit)):
+                run()
+                for other in ahead[2 * i : 2 * i + 2]:
+                    other()
+            if u == 1:
+                if gate < 2:
+                    load_gate(2, gate, [2, 2])
+                elif gate == 2:
+                    load_gate(3, 0, [2, 2])
+                else:
+                    load_gate(3, 1, [2, 1, 1])
+            if u == 3:
+                for nb in range(2):
+                    copy = nc.vector.tensor_copy if nb == 0 else nc.scalar.copy
+                    col = gate * HID + nb * BANK
+                    copy(out=hh_sb[:, col : col + BANK], in_=hh[(gate, nb)][:])
+
+        def mx_pass(acc, g, words, col):
+            k = 4 * (g % 4)
+            nc.tensor.matmul_mx(
+                out=acc[:],
+                lhsT=x_codes[:, P * g : P * (g + 1)].bitcast(FP8X4),
+                lhsT_scale=x_scales[:, P * g : P * (g + 1)],
+                rhs=words.bitcast(FP8X4),
+                rhs_scale=planes[k:P, g // 4, col : col + BANK],
+                start=(g == 0),
+                stop=(g == PASSES - 1),
+            )
+
+        def activate(acc, col, func, dst):
+            pre = work.tile([P, BANK], F32, name="pre", tag="pre")
+            nc.vector.tensor_tensor(out=pre[:], in0=acc[:], in1=hh_sb[:, col : col + BANK], op=ALU.add)
+            nc.scalar.activation(out=dst, in_=pre[:], func=func)
+
+        sig_i = keep.tile([P, HID], F32, name="sig_i")
+        sig_f = keep.tile([P, HID], F32, name="sig_f")
+        tanh_g = keep.tile([P, HID], F32, name="tanh_g")
+        c_new = keep.tile([P, HID], F32, name="c_new")
+        tanh_c = keep.tile([P, HID], F32, name="tanh_c")
+        sig_o = keep.tile([P, HID], F32, name="sig_o")
+
+        acc_if = [psum.tile([P, BANK], F32, name="acc_if", tag="tp") for b in range(4)]
+        for g in range(PASSES):
+            for b in range(4):
+                mx_pass(acc_if[b], g, w_if[g // 2][:, g % 2, b * BANK : (b + 1) * BANK], b * BANK)
+        for b in range(4):
+            dst = sig_i if b < 2 else sig_f
+            cols = slice((b % 2) * BANK, (b % 2 + 1) * BANK)
+            activate(acc_if[b], b * BANK, ACT.Sigmoid, dst[:, cols])
+        for nb in range(2):
+            cols = slice(nb * BANK, (nb + 1) * BANK)
+            nc.vector.tensor_tensor(out=sig_f[:, cols], in0=sig_f[:, cols], in1=c_sb[:, cols], op=ALU.mult)
+
+        def gate_passes(gate):
+            accs = [psum.tile([P, BANK], F32, name="acc_go", tag="acc") for nb in range(2)]
+            for g in range(PASSES):
+                for nb in range(2):
+                    mx_pass(
+                        accs[nb],
+                        g,
+                        w_go[(gate, g // 4)][:, g % 4, nb * BANK : (nb + 1) * BANK],
+                        gate * HID + nb * BANK,
+                    )
+            return accs
+
+        acc_g = gate_passes(2)
+        for nb in range(2):
+            cols = slice(nb * BANK, (nb + 1) * BANK)
+            activate(acc_g[nb], 2 * HID + nb * BANK, ACT.Tanh, tanh_g[:, cols])
+            nc.vector.tensor_tensor(out=tanh_g[:, cols], in0=tanh_g[:, cols], in1=sig_i[:, cols], op=ALU.mult)
+            nc.vector.tensor_tensor(out=c_new[:, cols], in0=tanh_g[:, cols], in1=sig_f[:, cols], op=ALU.add)
+            nc.scalar.activation(out=tanh_c[:, cols], in_=c_new[:, cols], func=ACT.Tanh)
+        nc.sync.dma_start(out=out_1, in_=c_new[:])
+
+        acc_o = gate_passes(3)
+        for nb in range(2):
+            cols = slice(nb * BANK, (nb + 1) * BANK)
+            activate(acc_o[nb], 3 * HID + nb * BANK, ACT.Sigmoid, sig_o[:, cols])
+            nc.vector.tensor_tensor(out=sig_o[:, cols], in0=sig_o[:, cols], in1=tanh_c[:, cols], op=ALU.mult)
+            nc.sync.dma_start(out=out_0[:, cols], in_=sig_o[:, cols])

@@ -72,9 +72,9 @@ def tile_int8lstmcell_w_kernel(
 
         ww = w_ih_words.rearrange("g p n t -> g p (n t)").bitcast(I32)
 
-        def load_w(dst, first_local, first_pass, n_pass, col, n_col):
+        def load_w(dst, first_local, first_pass, n_pass, col, n_col, dst_col=0):
             nc.sync.dma_start(
-                out=dst[:, first_local : first_local + n_pass, :].bitcast(I32),
+                out=dst[:, first_local : first_local + n_pass, dst_col : dst_col + n_col].bitcast(I32),
                 in_=ww[first_pass : first_pass + n_pass, :, col : col + n_col].rearrange("g p n -> p g n"),
             )
 
@@ -94,6 +94,9 @@ def tile_int8lstmcell_w_kernel(
             for n_pass in cuts:
                 load_w(dst, first, 4 * j + first, n_pass, gate * HID, HID)
                 first += n_pass
+            if first < 4:
+                for nb in range(2):
+                    load_w(dst, first, 4 * j + first, 1, gate * HID + nb * BANK, BANK, nb * BANK)
             w_go[(gate, j)] = dst
 
         for j in range(3):
@@ -210,7 +213,7 @@ def tile_int8lstmcell_w_kernel(
                 elif gate == 2:
                     load_gate(3, 0, [2, 2])
                 else:
-                    load_gate(3, 1, [2, 1, 1])
+                    load_gate(3, 1, [2, 1])
             if u == 3:
                 for nb in range(2):
                     copy = nc.vector.tensor_copy if nb == 0 else nc.scalar.copy
@@ -229,10 +232,15 @@ def tile_int8lstmcell_w_kernel(
                 stop=(g == PASSES - 1),
             )
 
-        def activate(acc, col, func, dst):
-            pre = work.tile([P, BANK], F32, name="pre", tag="pre")
-            nc.vector.tensor_tensor(out=pre[:], in0=acc[:], in1=hh_sb[:, col : col + BANK], op=ALU.add)
-            nc.scalar.activation(out=dst, in_=pre[:], func=func)
+        def activate(accs, col, func, dst):
+            pres = []
+            for b, acc in enumerate(accs):
+                pre = work.tile([P, BANK], F32, name="pre", tag="pre")
+                first = col + b * BANK
+                nc.vector.tensor_tensor(out=pre[:], in0=acc[:], in1=hh_sb[:, first : first + BANK], op=ALU.add)
+                pres.append(pre)
+            for b, pre in enumerate(pres):
+                nc.scalar.activation(out=dst[:, b * BANK : (b + 1) * BANK], in_=pre[:], func=func)
 
         sig_i = keep.tile([P, HID], F32, name="sig_i")
         sig_f = keep.tile([P, HID], F32, name="sig_f")
@@ -245,10 +253,8 @@ def tile_int8lstmcell_w_kernel(
         for g in range(PASSES):
             for b in range(4):
                 mx_pass(acc_if[b], g, w_if[g // 2][:, g % 2, b * BANK : (b + 1) * BANK], b * BANK)
-        for b in range(4):
-            dst = sig_i if b < 2 else sig_f
-            cols = slice((b % 2) * BANK, (b % 2 + 1) * BANK)
-            activate(acc_if[b], b * BANK, ACT.Sigmoid, dst[:, cols])
+        activate(acc_if[0:2], 0, ACT.Sigmoid, sig_i)
+        activate(acc_if[2:4], HID, ACT.Sigmoid, sig_f)
         for nb in range(2):
             cols = slice(nb * BANK, (nb + 1) * BANK)
             nc.vector.tensor_tensor(out=sig_f[:, cols], in0=sig_f[:, cols], in1=c_sb[:, cols], op=ALU.mult)
@@ -266,17 +272,17 @@ def tile_int8lstmcell_w_kernel(
             return accs
 
         acc_g = gate_passes(2)
+        activate(acc_g, 2 * HID, ACT.Tanh, tanh_g)
         for nb in range(2):
             cols = slice(nb * BANK, (nb + 1) * BANK)
-            activate(acc_g[nb], 2 * HID + nb * BANK, ACT.Tanh, tanh_g[:, cols])
             nc.vector.tensor_tensor(out=tanh_g[:, cols], in0=tanh_g[:, cols], in1=sig_i[:, cols], op=ALU.mult)
             nc.vector.tensor_tensor(out=c_new[:, cols], in0=tanh_g[:, cols], in1=sig_f[:, cols], op=ALU.add)
             nc.scalar.activation(out=tanh_c[:, cols], in_=c_new[:, cols], func=ACT.Tanh)
         nc.sync.dma_start(out=out_1, in_=c_new[:])
 
         acc_o = gate_passes(3)
+        activate(acc_o, 3 * HID, ACT.Sigmoid, sig_o)
         for nb in range(2):
             cols = slice(nb * BANK, (nb + 1) * BANK)
-            activate(acc_o[nb], 3 * HID + nb * BANK, ACT.Sigmoid, sig_o[:, cols])
             nc.vector.tensor_tensor(out=sig_o[:, cols], in0=sig_o[:, cols], in1=tanh_c[:, cols], op=ALU.mult)
             nc.sync.dma_start(out=out_0[:, cols], in_=sig_o[:, cols])

@@ -53,8 +53,8 @@ def tile_int8lstmcell_w_kernel(
         nc.sync.dma_start(out=bias_rows[0:8, :], in_=bias_ih.rearrange("(j n) -> j n", j=8))
         nc.sync.dma_start(out=bias_rows[8:16, :], in_=bias_hh.rearrange("(j n) -> j n", j=8))
         scale_words = w_ih_scales.bitcast(I32)
-        for t in range(2):
-            for q in range(4):
+        for q in (2, 3, 0, 1):
+            for t in range(2):
                 nc.sync.dma_start(
                     out=planes[32 * q : 32 * q + 16, t, :].bitcast(I32),
                     in_=scale_words[4 * t : 4 * t + 4, 4 * q : 4 * q + 4, :],

@@ -203,10 +203,10 @@ def tile_int8lstmcell_w_kernel(
                         stop=False,
                     )
             ahead = transpose_steps(unit + 2) if unit + 2 < 4 * GATES else []
-            for i, run in enumerate(matmul_steps(unit)):
+            for run in matmul_steps(unit):
                 run()
-                for other in ahead[2 * i : 2 * i + 2]:
-                    other()
+            for other in ahead:
+                other()
             if u == 1:
                 if gate < 2:
                     load_gate(2, gate, [2, 2])

@@ -22,6 +22,7 @@ BANK = 512
 FLOPS = 2 * BATCH * (IN + HID) * GATES * HID
 
 MANUAL = True
+LAST = 256
 
 
 def tile_int8lstmcell_w_kernel(
@@ -98,6 +99,17 @@ def tile_int8lstmcell_w_kernel(
                 for nb in range(2):
                     load_w(dst, first, 4 * j + first, 1, gate * HID + nb * BANK, BANK, nb * BANK)
             w_go[(gate, j)] = dst
+
+        def load_last():
+            dst = big.tile([P, 4, HID], U32, name="w_go", tag="big", align_bytes=64)
+            col = 3 * HID
+            load_w(dst, 0, 4, 2, col, BANK)
+            load_w(dst, 2, 6, 2, col, BANK)
+            load_w(dst, 0, 4, 2, col + BANK, BANK, BANK)
+            load_w(dst, 2, 6, 2, col + BANK, LAST, BANK)
+            load_w(dst, 2, 6, 1, col + BANK + LAST, LAST, BANK + LAST)
+            load_w(dst, 3, 7, 1, col + BANK + LAST, LAST, BANK + LAST)
+            w_go[(3, 1)] = dst
 
         for j in range(3):
             load_if(j)
@@ -213,21 +225,21 @@ def tile_int8lstmcell_w_kernel(
                 elif gate == 2:
                     load_gate(3, 0, [2, 2])
                 else:
-                    load_gate(3, 1, [2, 1])
+                    load_last()
             if u == 3:
                 for nb in range(2):
                     copy = nc.vector.tensor_copy if nb == 0 else nc.scalar.copy
                     col = gate * HID + nb * BANK
                     copy(out=hh_sb[:, col : col + BANK], in_=hh[(gate, nb)][:])
 
-        def mx_pass(acc, g, words, col):
+        def mx_pass(acc, g, words, col, width=BANK):
             k = 4 * (g % 4)
             nc.tensor.matmul_mx(
-                out=acc[:],
+                out=acc[:, 0:width],
                 lhsT=x_codes[:, P * g : P * (g + 1)].bitcast(FP8X4),
                 lhsT_scale=x_scales[:, P * g : P * (g + 1)],
                 rhs=words.bitcast(FP8X4),
-                rhs_scale=planes[k:P, g // 4, col : col + BANK],
+                rhs_scale=planes[k:P, g // 4, col : col + width],
                 start=(g == 0),
                 stop=(g == PASSES - 1),
             )
@@ -280,9 +292,44 @@ def tile_int8lstmcell_w_kernel(
             nc.scalar.activation(out=tanh_c[:, cols], in_=c_new[:, cols], func=ACT.Tanh)
         nc.sync.dma_start(out=out_1, in_=c_new[:])
 
-        acc_o = gate_passes(3)
-        activate(acc_o, 3 * HID, ACT.Sigmoid, sig_o)
-        for nb in range(2):
-            cols = slice(nb * BANK, (nb + 1) * BANK)
+        pieces = [(0, BANK), (BANK, LAST), (BANK + LAST, LAST)]
+        acc_o = [
+            psum.tile([P, BANK], F32, name="acc_o", tag="acc"),
+            psum.tile([P, BANK], F32, name="acc_o", tag="tp"),
+            psum.tile([P, BANK], F32, name="acc_o", tag="tp"),
+        ]
+
+        def o_passes(i, first, stop_at):
+            col, width = pieces[i]
+            for g in range(first, stop_at):
+                mx_pass(acc_o[i], g, w_go[(3, g // 4)][:, g % 4, col : col + width], 3 * HID + col, width)
+
+        def o_add(i):
+            col, width = pieces[i]
+            pre = work.tile([P, BANK], F32, name="pre", tag="pre")
+            nc.vector.tensor_tensor(
+                out=pre[:, 0:width],
+                in0=acc_o[i][:, 0:width],
+                in1=hh_sb[:, 3 * HID + col : 3 * HID + col + width],
+                op=ALU.add,
+            )
+            nc.scalar.activation(out=sig_o[:, col : col + width], in_=pre[:, 0:width], func=ACT.Sigmoid)
+
+        def o_out(i):
+            col, width = pieces[i]
+            cols = slice(col, col + width)
             nc.vector.tensor_tensor(out=sig_o[:, cols], in0=sig_o[:, cols], in1=tanh_c[:, cols], op=ALU.mult)
             nc.sync.dma_start(out=out_0[:, cols], in_=sig_o[:, cols])
+
+        for i in range(3):
+            o_passes(i, 0, 4)
+        o_passes(0, 4, PASSES)
+        o_add(0)
+        o_passes(1, 4, 6)
+        o_passes(2, 4, 6)
+        o_passes(1, 6, PASSES)
+        o_passes(2, 6, PASSES)
+        o_add(1)
+        o_add(2)
+        for i in range(3):
+            o_out(i)

@@ -83,8 +83,7 @@ def tile_int8lstmcell_w_kernel(
 
         def load_if(j):
             dst = big.tile([P, 2, 2 * HID], U32, name="w_if", tag="big", align_bytes=64)
-            load_w(dst, 0, 2 * j, 1, 0, 2 * HID)
-            load_w(dst, 1, 2 * j + 1, 1, 0, 2 * HID)
+            load_w(dst, 0, 2 * j, 2, 0, 2 * HID)
             w_if.append(dst)
 
         w_go = {}
@@ -221,7 +220,7 @@ def tile_int8lstmcell_w_kernel(
                 other()
             if u == 1:
                 if gate < 2:
-                    load_gate(2, gate, [2, 2])
+                    load_gate(2, gate, [4])
                 elif gate == 2:
                     load_gate(3, 0, [2, 2])
                 else:

from contextlib import ExitStack

import concourse.mybir as mybir
from concourse.masks import make_identity

F32 = mybir.dt.float32
BF16 = mybir.dt.bfloat16
I32 = mybir.dt.int32
U32 = mybir.dt.uint32
U8 = mybir.dt.uint8
FP8X4 = mybir.dt.float8_e4m3fn_x4
ACT = mybir.ActivationFunctionType
ALU = mybir.AluOpType

P = 128
BATCH = 128
IN = 4096
HID = 1024
GATES = 4
PASSES = IN // 512
BANK = 512
FLOPS = 2 * BATCH * (IN + HID) * GATES * HID

MANUAL = True
LAST = 256


def tile_int8lstmcell_w_kernel(
    tc, x, h_prev, c_prev, w_ih_words, w_ih_scales, w_hh, bias_ih, bias_hh, out_0, out_1
):
    nc = tc.nc
    with ExitStack() as stack:
        if MANUAL:
            stack.enter_context(tc.manual_schedule())
        keep = stack.enter_context(tc.tile_pool(name="keep", bufs=1))
        big = stack.enter_context(tc.tile_pool(name="big", bufs=8))
        turned = stack.enter_context(tc.tile_pool(name="turned", bufs=5))
        work = stack.enter_context(tc.tile_pool(name="work", bufs=3))
        psum = stack.enter_context(tc.psum_pool(name="psum", bufs=4))

        planes = keep.tile([P, 2, IN], U8, name="planes", align_bytes=64)
        nc.vector.memset(planes[:].rearrange("p t n -> p (t n)").bitcast(I32), 0)
        bias_rows = keep.tile([P, BANK], BF16, name="bias_rows")
        nc.vector.memset(bias_rows[:], 0.0)
        ident = keep.tile([P, P], F32, name="ident")
        make_identity(nc, ident[:])
        pick = keep.tile([P, 8], BF16, name="pick")
        nc.vector.tensor_tensor(out=pick[:], in0=ident[:, 0:8], in1=ident[:, 8:16], op=ALU.add)

        h_sb = keep.tile([P, HID], BF16, name="h_sb")
        nc.sync.dma_start(out=h_sb[:], in_=h_prev)
        x_sb = big.tile([P, IN], BF16, name="x_sb", tag="big", align_bytes=64)
        nc.sync.dma_start(out=x_sb[:], in_=x)
        nc.sync.dma_start(out=bias_rows[0:8, :], in_=bias_ih.rearrange("(j n) -> j n", j=8))
        nc.sync.dma_start(out=bias_rows[8:16, :], in_=bias_hh.rearrange("(j n) -> j n", j=8))
        scale_words = w_ih_scales.bitcast(I32)
        for q in (2, 3, 0, 1):
            for t in range(2):
                nc.sync.dma_start(
                    out=planes[32 * q : 32 * q + 16, t, :].bitcast(I32),
                    in_=scale_words[4 * t : 4 * t + 4, 4 * q : 4 * q + 4, :],
                )
        w_words = []
        for gate in range(GATES):
            w_nat = big.tile([P, 8 * HID], BF16, name="w_nat", tag="big", align_bytes=64)
            nc.sync.dma_start(
                out=w_nat[:],
                in_=w_hh[gate * HID : (gate + 1) * HID, :].rearrange("(p a) k -> p (a k)", a=8),
            )
            w_words.append(w_nat[:].bitcast(F32))
        c_sb = keep.tile([P, HID], BF16, name="c_sb")
        nc.sync.dma_start(out=c_sb[:], in_=c_prev)

        ww = w_ih_words.rearrange("g p n t -> g p (n t)").bitcast(I32)

        def load_w(dst, first_local, first_pass, n_pass, col, n_col, dst_col=0):
            nc.sync.dma_start(
                out=dst[:, first_local : first_local + n_pass, dst_col : dst_col + n_col].bitcast(I32),
                in_=ww[first_pass : first_pass + n_pass, :, col : col + n_col].rearrange("g p n -> p g n"),
            )

        w_if = []

        def load_if(j):
            dst = big.tile([P, 2, 2 * HID], U32, name="w_if", tag="big", align_bytes=64)
            load_w(dst, 0, 2 * j, 2, 0, 2 * HID)
            w_if.append(dst)

        w_go = {}

        def load_gate(gate, j, cuts):
            dst = big.tile([P, 4, HID], U32, name="w_go", tag="big", align_bytes=64)
            first = 0
            for n_pass in cuts:
                load_w(dst, first, 4 * j + first, n_pass, gate * HID, HID)
                first += n_pass
            if first < 4:
                for nb in range(2):
                    load_w(dst, first, 4 * j + first, 1, gate * HID + nb * BANK, BANK, nb * BANK)
            w_go[(gate, j)] = dst

        def load_last():
            dst = big.tile([P, 4, HID], U32, name="w_go", tag="big", align_bytes=64)
            col = 3 * HID
            load_w(dst, 0, 4, 2, col, BANK)
            load_w(dst, 2, 6, 2, col, BANK)
            load_w(dst, 0, 4, 2, col + BANK, BANK, BANK)
            load_w(dst, 2, 6, 2, col + BANK, LAST, BANK)
            load_w(dst, 2, 6, 1, col + BANK + LAST, LAST, BANK + LAST)
            load_w(dst, 3, 7, 1, col + BANK + LAST, LAST, BANK + LAST)
            w_go[(3, 1)] = dst

        for j in range(3):
            load_if(j)

        h_words = h_sb[:].bitcast(F32)
        h_bank = psum.tile([P, 4, P], F32, name="h_bank", tag="tp")
        for u in range(4):
            nc.tensor.transpose(out=h_bank[:, u, :], in_=h_words[:, P * u : P * (u + 1)], identity=ident[:])
        h_t = keep.tile([P, 4, 2, P], BF16, name="h_t")
        nc.vector.tensor_copy(
            out=h_t[:],
            in_=h_bank[:].rearrange("q u b -> q (u b)").bitcast(BF16).rearrange("q (u b e) -> q u e b", u=4, e=2),
        )

        x_words = x_sb[:].bitcast(F32)
        x_codes = keep.tile([P, PASSES * P], U32, name="x_codes", align_bytes=64)
        x_scales = keep.tile([P, PASSES * P], U8, name="x_scales", align_bytes=64)
        grouped = []
        for half in range(2):
            grp = turned.tile([P, 4, P, 2], F32, name="grp", tag="turned", align_bytes=64)
            for pair in range(2):
                x_bank = psum.tile([P, 2, 2, P], F32, name="x_bank", tag="tp")
                for gl in range(2):
                    g = 4 * half + 2 * pair + gl
                    for u in range(2):
                        nc.tensor.transpose(
                            out=x_bank[:, gl, u, :],
                            in_=x_words[:, 256 * g + u : 256 * (g + 1) : 2],
                            identity=ident[:],
                        )
                copy = nc.vector.tensor_copy if pair == 0 else nc.scalar.copy
                copy(out=grp[:, 2 * pair : 2 * pair + 2, :, :], in_=x_bank[:].rearrange("p g u b -> p g b u"))
            grouped.append(grp)
        for half in range(2):
            nc.vector.quantize_mx(
                out=x_codes[:, 512 * half : 512 * (half + 1)].bitcast(FP8X4),
                scales=x_scales[:, 512 * half : 512 * (half + 1)],
                in_=grouped[half][:].rearrange("p g b u -> p (g b u)").bitcast(BF16),
            )
        load_if(3)

        hh_sb = keep.tile([P, GATES * HID], F32, name="hh_sb")
        w_t = {}
        hh = {}

        def transpose_steps(unit):
            gate, u = divmod(unit, 4)
            copy = nc.vector.tensor_copy if unit % 2 == 0 else nc.scalar.copy
            state = {}

            def step(half, a):
                def run():
                    if half == 0 and a == 0:
                        w_t[unit] = turned.tile([P, P, 8], F32, name="w_t", tag="turned", align_bytes=64)
                    if a == 0:
                        state["bank"] = psum.tile([P, 4, P], F32, name="w_bank", tag="tp")
                    first = (4 * half + a) * (HID // 2) + P * u
                    nc.tensor.transpose(
                        out=state["bank"][:, a, :], in_=w_words[gate][:, first : first + P], identity=ident[:]
                    )
                    if a == 3:
                        copy(
                            out=w_t[unit][:, :, 4 * half : 4 * half + 4],
                            in_=state["bank"][:].rearrange("q a p -> q p a"),
                        )

                return run

            return [step(half, a) for half in range(2) for a in range(4)]

        def matmul_steps(unit):
            gate, u = divmod(unit, 4)

            def step(e, nb):
                def run():
                    pairs = w_t[unit][:].rearrange("q p a -> q (p a)").bitcast(BF16)
                    nc.tensor.matmul(
                        out=hh[(gate, nb)][:],
                        lhsT=h_t[:, u, e, :],
                        rhs=pairs.rearrange("q (n e) -> q n e", e=2)[:, nb * BANK : (nb + 1) * BANK, e],
                        start=False,
                        stop=(u == 3 and e == 1),
                    )

                return run

            return [step(e, nb) for e in range(2) for nb in range(2)]

        for unit in range(2):
            for run in transpose_steps(unit):
                run()
        for unit in range(4 * GATES):
            gate, u = divmod(unit, 4)
            if u == 0:
                for nb in range(2):
                    hh[(gate, nb)] = psum.tile([P, BANK], F32, name="hh", tag="acc")
                    j = 2 * gate + nb
                    nc.tensor.matmul(
                        out=hh[(gate, nb)][:],
                        lhsT=pick[:, j : j + 1].to_broadcast([P, P]),
                        rhs=bias_rows[:],
                        start=True,
                        stop=False,
                    )
            ahead = transpose_steps(unit + 2) if unit + 2 < 4 * GATES else []
            for run in matmul_steps(unit):
                run()
            for other in ahead:
                other()
            if u == 1:
                if gate < 2:
                    load_gate(2, gate, [4])
                elif gate == 2:
                    load_gate(3, 0, [2, 2])
                else:
                    load_last()
            if u == 3:
                for nb in range(2):
                    copy = nc.vector.tensor_copy if nb == 0 else nc.scalar.copy
                    col = gate * HID + nb * BANK
                    copy(out=hh_sb[:, col : col + BANK], in_=hh[(gate, nb)][:])

        def mx_pass(acc, g, words, col, width=BANK):
            k = 4 * (g % 4)
            nc.tensor.matmul_mx(
                out=acc[:, 0:width],
                lhsT=x_codes[:, P * g : P * (g + 1)].bitcast(FP8X4),
                lhsT_scale=x_scales[:, P * g : P * (g + 1)],
                rhs=words.bitcast(FP8X4),
                rhs_scale=planes[k:P, g // 4, col : col + width],
                start=(g == 0),
                stop=(g == PASSES - 1),
            )

        def activate(accs, col, func, dst):
            pres = []
            for b, acc in enumerate(accs):
                pre = work.tile([P, BANK], F32, name="pre", tag="pre")
                first = col + b * BANK
                nc.vector.tensor_tensor(out=pre[:], in0=acc[:], in1=hh_sb[:, first : first + BANK], op=ALU.add)
                pres.append(pre)
            for b, pre in enumerate(pres):
                nc.scalar.activation(out=dst[:, b * BANK : (b + 1) * BANK], in_=pre[:], func=func)

        sig_i = keep.tile([P, HID], F32, name="sig_i")
        sig_f = keep.tile([P, HID], F32, name="sig_f")
        tanh_g = keep.tile([P, HID], F32, name="tanh_g")
        c_new = keep.tile([P, HID], F32, name="c_new")
        tanh_c = keep.tile([P, HID], F32, name="tanh_c")
        sig_o = keep.tile([P, HID], F32, name="sig_o")

        acc_if = [psum.tile([P, BANK], F32, name="acc_if", tag="tp") for b in range(4)]
        for g in range(PASSES):
            for b in range(4):
                mx_pass(acc_if[b], g, w_if[g // 2][:, g % 2, b * BANK : (b + 1) * BANK], b * BANK)
        activate(acc_if[0:2], 0, ACT.Sigmoid, sig_i)
        activate(acc_if[2:4], HID, ACT.Sigmoid, sig_f)
        for nb in range(2):
            cols = slice(nb * BANK, (nb + 1) * BANK)
            nc.vector.tensor_tensor(out=sig_f[:, cols], in0=sig_f[:, cols], in1=c_sb[:, cols], op=ALU.mult)

        def gate_passes(gate):
            accs = [psum.tile([P, BANK], F32, name="acc_go", tag="acc") for nb in range(2)]
            for g in range(PASSES):
                for nb in range(2):
                    mx_pass(
                        accs[nb],
                        g,
                        w_go[(gate, g // 4)][:, g % 4, nb * BANK : (nb + 1) * BANK],
                        gate * HID + nb * BANK,
                    )
            return accs

        acc_g = gate_passes(2)
        activate(acc_g, 2 * HID, ACT.Tanh, tanh_g)
        for nb in range(2):
            cols = slice(nb * BANK, (nb + 1) * BANK)
            nc.vector.tensor_tensor(out=tanh_g[:, cols], in0=tanh_g[:, cols], in1=sig_i[:, cols], op=ALU.mult)
            nc.vector.tensor_tensor(out=c_new[:, cols], in0=tanh_g[:, cols], in1=sig_f[:, cols], op=ALU.add)
            nc.scalar.activation(out=tanh_c[:, cols], in_=c_new[:, cols], func=ACT.Tanh)
        nc.sync.dma_start(out=out_1, in_=c_new[:])

        pieces = [(0, BANK), (BANK, LAST), (BANK + LAST, LAST)]
        acc_o = [
            psum.tile([P, BANK], F32, name="acc_o", tag="acc"),
            psum.tile([P, BANK], F32, name="acc_o", tag="tp"),
            psum.tile([P, BANK], F32, name="acc_o", tag="tp"),
        ]

        def o_passes(i, first, stop_at):
            col, width = pieces[i]
            for g in range(first, stop_at):
                mx_pass(acc_o[i], g, w_go[(3, g // 4)][:, g % 4, col : col + width], 3 * HID + col, width)

        def o_add(i):
            col, width = pieces[i]
            pre = work.tile([P, BANK], F32, name="pre", tag="pre")
            nc.vector.tensor_tensor(
                out=pre[:, 0:width],
                in0=acc_o[i][:, 0:width],
                in1=hh_sb[:, 3 * HID + col : 3 * HID + col + width],
                op=ALU.add,
            )
            nc.scalar.activation(out=sig_o[:, col : col + width], in_=pre[:, 0:width], func=ACT.Sigmoid)

        def o_out(i):
            col, width = pieces[i]
            cols = slice(col, col + width)
            nc.vector.tensor_tensor(out=sig_o[:, cols], in0=sig_o[:, cols], in1=tanh_c[:, cols], op=ALU.mult)
            nc.sync.dma_start(out=out_0[:, cols], in_=sig_o[:, cols])

        for i in range(3):
            o_passes(i, 0, 4)
        o_passes(0, 4, PASSES)
        o_add(0)
        o_passes(1, 4, 6)
        o_passes(2, 4, 6)
        o_passes(1, 6, PASSES)
        o_passes(2, 6, PASSES)
        o_add(1)
        o_add(2)
        for i in range(3):
            o_out(i)
